import numpy as np
import ml_dtypes


def mxq(x, axis, fmt="e4m3"):
    dtype, down = {"e4m3": (ml_dtypes.float8_e4m3fn, 7), "e5m2": (ml_dtypes.float8_e5m2, 14)}[fmt]
    v = np.moveaxis(np.asarray(x, np.float32).astype(ml_dtypes.bfloat16).astype(np.float64), axis, -1)
    blocks = v.reshape(v.shape[:-1] + (-1, 32))
    amax = np.abs(blocks).max(-1, keepdims=True)
    byte = np.maximum(np.where(amax > 0, np.frexp(amax)[1] - 1 + 127, 0) - down, 1)
    scale = np.exp2(byte - 127.0)
    codes = (blocks / scale).astype(np.float32).astype(dtype).astype(np.float64)
    return np.moveaxis((codes * scale).reshape(v.shape), -1, axis)


WIDE = False


def mx_kscale(k):
    if not WIDE:
        return np.ones(k)
    levels = np.array([10, -10, 5, -5, 0])
    a = np.random.permutation(np.resize(levels, k // 512 * 4)).reshape(k // 512, 4)
    idx = np.arange(k)
    return np.exp2(a[idx // 512, idx % 128 // 32])


BF16 = ml_dtypes.bfloat16


def bf(x):
    return np.asarray(x, np.float32).astype(BF16)


def f64(x):
    return np.asarray(x).astype(np.float64)


B, L, EMB, HD, NH = 2, 128, 8192, 128, 8
THETA = 10000.0


def rope_mats(seq_len):
    freqs = 1.0 / THETA ** (f64(np.arange(0, HD, 2)) / HD)
    t = f64(np.arange(seq_len))
    f = np.repeat(t[:, None] * freqs[None, :], 2, axis=-1)
    return np.cos(f), np.sin(f)


def apply_rope(u, rc, rs):
    ue = u[..., 0::2]
    uo = u[..., 1::2]
    u_rot = np.stack([-uo, ue], axis=-1).reshape(u.shape)
    return u * rc + u_rot * rs


def setup_inputs():
    s = mx_kscale(EMB)
    w = 1.0 / np.sqrt(EMB)
    return {"x": bf(np.random.standard_normal((B, L, EMB)) * s),
            "Wq": bf(np.random.standard_normal((EMB, HD * NH)) * w / s[:, None]),
            "Wk": bf(np.random.standard_normal((EMB, HD)) * w / s[:, None]),
            "Wv": bf(np.random.standard_normal((EMB, HD)) * w / s[:, None])}


def reference(x, Wq, Wk, Wv):
    xq = mxq(f64(x), 2, "e4m3")
    Q = (xq @ mxq(f64(Wq), 0, "e4m3")).reshape(B, L, NH, HD).transpose(0, 2, 1, 3)
    K = xq @ mxq(f64(Wk), 0, "e4m3")
    V = xq @ mxq(f64(Wv), 0, "e4m3")
    rc, rs = rope_mats(L)
    return apply_rope(Q, rc, rs), apply_rope(K, rc, rs), V

@@ -1,0 +1,278 @@
+import math
+from contextlib import ExitStack
+
+import concourse.mybir as mybir
+from concourse.masks import make_identity
+
+F32 = mybir.dt.float32
+BF16 = mybir.dt.bfloat16
+I32 = mybir.dt.int32
+U32 = mybir.dt.uint32
+U8 = mybir.dt.uint8
+FP8X4 = mybir.dt.float8_e4m3fn_x4
+ALU = mybir.AluOpType
+ACT = mybir.ActivationFunctionType
+
+BATCH, SEQ, EMB, HEAD_DIM, Q_HEADS = 2, 128, 8192, 128, 8
+THETA = 10000.0
+PAIRS = HEAD_DIM // 2
+PAIR_BITS = 6
+
+P = 128
+PACK = 4
+K_PASS = P * PACK
+PASSES = EMB // K_PASS
+BANK = 512
+UNIT = 1024
+GROUP = 4
+CHUNKS = PASSES // GROUP
+RUN = 4
+WQ_AHEAD = 6
+ROUND = 1.5 * 2.0**23
+
+FLOPS = 2 * BATCH * SEQ * EMB * (Q_HEADS + 2) * HEAD_DIM
+
+assert 2**PAIR_BITS == PAIRS
+assert GROUP * BATCH * SEQ == UNIT and GROUP * 2 * HEAD_DIM == UNIT and Q_HEADS * HEAD_DIM == UNIT
+assert BATCH * UNIT // BANK == CHUNKS
+assert CHUNKS <= WQ_AHEAD
+
+
+def tile_groupropeattention_pa_k_kernel(tc, x, Wq, Wk, Wv, out_0, out_1, out_2):
+    nc = tc.nc
+    with ExitStack() as ctx:
+        ctx.enter_context(tc.manual_schedule())
+        const = ctx.enter_context(tc.tile_pool(name="const", bufs=1))
+        narrow_in = ctx.enter_context(tc.tile_pool(name="narrow_in", bufs=2 * CHUNKS))
+        wide_in = ctx.enter_context(tc.tile_pool(name="wide_in", bufs=WQ_AHEAD))
+        grouped_pool = ctx.enter_context(tc.tile_pool(name="grouped", bufs=3))
+        mx_pool = ctx.enter_context(tc.tile_pool(name="mx", bufs=3))
+        rope_pool = ctx.enter_context(tc.tile_pool(name="rope", bufs=2))
+        q_banks = ctx.enter_context(tc.psum_pool(name="q_banks", bufs=1))
+        spare_banks = ctx.enter_context(tc.psum_pool(name="spare_banks", bufs=4))
+
+        position = const.tile([P, 1], I32, name="position")
+        nc.gpsimd.iota(position[:], pattern=[[0, 1]], base=0, channel_multiplier=1)
+        ident = const.tile([P, P], F32, name="ident")
+        make_identity(nc, ident[:])
+
+        position_turns = const.tile([P, 1], F32, name="position_turns")
+        nc.vector.tensor_scalar_mul(out=position_turns[:], in0=position[:], scalar1=1.0 / (2.0 * math.pi))
+        frequency = const.tile([P, PAIRS], F32, name="frequency")
+        nc.vector.memset(frequency[:], 1.0)
+        for level in range(PAIR_BITS):
+            bit = 2**level
+            bit_set = frequency[:].rearrange("p (a two s) -> p a two s", two=2, s=bit)[:, :, 1, :]
+            nc.vector.tensor_scalar_mul(out=bit_set, in0=bit_set, scalar1=THETA ** (-bit / PAIRS))
+        turns = const.tile([P, 3, PAIRS], F32, name="turns")
+        for row, shift in enumerate((0.25, 0.0, 0.5)):
+            nc.vector.tensor_scalar(
+                out=turns[:, row, :],
+                in0=frequency[:],
+                scalar1=position_turns[:, 0:1],
+                scalar2=shift,
+                op0=ALU.mult,
+                op1=ALU.add,
+            )
+        whole_turns = const.tile([P, 3, PAIRS], F32, name="whole_turns")
+        nc.vector.tensor_scalar(
+            out=whole_turns[:], in0=turns[:], scalar1=ROUND, scalar2=ROUND, op0=ALU.add, op1=ALU.subtract
+        )
+        nc.vector.tensor_tensor(out=turns[:], in0=turns[:], in1=whole_turns[:], op=ALU.subtract)
+        trig = const.tile([P, 3, PAIRS], F32, name="trig")
+        nc.scalar.activation(out=trig[:], in_=turns[:], func=ACT.Sin, scale=2.0 * math.pi)
+        cos, sin, minus_sin = trig[:, 0, :], trig[:, 1, :], trig[:, 2, :]
+
+        def quantise(grouped, codes, scales):
+            nc.vector.quantize_mx(out=codes.bitcast(FP8X4), scales=scales, in_=grouped)
+
+        def quantise_weights(grouped):
+            codes = mx_pool.tile([P, UNIT], U32, name="w_codes", align_bytes=64)
+            scales = mx_pool.tile([P, UNIT], U8, name="w_scales", align_bytes=64)
+            quantise(grouped[:].rearrange("p n j -> p (n j)"), codes[:], scales[:])
+            return codes, scales
+
+        def regroup(copy, grouped_cols, raw_cols):
+            copy(
+                out=grouped_cols.rearrange("p (c i) j -> p c j i", i=RUN),
+                in_=raw_cols.rearrange("p j (c i) -> p c j i", i=RUN),
+            )
+
+        def multiply(acc, c, b, codes, scales, cols):
+            tokens = slice((c * BATCH + b) * SEQ, (c * BATCH + b + 1) * SEQ)
+            nc.tensor.matmul_mx(
+                out=acc[:],
+                lhsT=x_codes[:, tokens].bitcast(FP8X4),
+                lhsT_scale=x_scales[:, tokens],
+                rhs=codes[:, cols].bitcast(FP8X4),
+                rhs_scale=scales[:, cols],
+                start=(c == 0),
+                stop=(c == PASSES - 1),
+            )
+
+        def rope_and_store(acc, heads, out_rows):
+            pairs = acc[:].rearrange("p (h k two) -> p h k two", h=heads, two=2)
+            direct = rope_pool.tile([P, heads, PAIRS, 2], F32, name="direct")
+            nc.vector.tensor_tensor(
+                out=direct[:],
+                in0=pairs,
+                in1=cos.unsqueeze(1).unsqueeze(3).to_broadcast([P, heads, PAIRS, 2]),
+                op=ALU.mult,
+            )
+            crossed = rope_pool.tile([P, heads, 2, PAIRS], F32, name="crossed")
+            nc.vector.tensor_tensor(
+                out=crossed[:, :, 0, :],
+                in0=pairs[:, :, :, 1],
+                in1=minus_sin.unsqueeze(1).to_broadcast([P, heads, PAIRS]),
+                op=ALU.mult,
+            )
+            nc.vector.tensor_tensor(
+                out=crossed[:, :, 1, :],
+                in0=pairs[:, :, :, 0],
+                in1=sin.unsqueeze(1).to_broadcast([P, heads, PAIRS]),
+                op=ALU.mult,
+            )
+            nc.vector.tensor_tensor(
+                out=direct[:], in0=direct[:], in1=crossed[:].rearrange("p h two k -> p h k two"), op=ALU.add
+            )
+            nc.sync.dma_start(out=out_rows, in_=direct[:].rearrange("p h k two -> p h (k two)"))
+
+        x_raw = []
+
+        def load_x(chunk):
+            for b in range(BATCH):
+                piece = narrow_in.tile([P, GROUP * K_PASS], BF16, name="x_raw", tag="narrow")
+                nc.sync.dma_start(out=piece[:], in_=x[b, :, chunk * GROUP * K_PASS : (chunk + 1) * GROUP * K_PASS])
+                x_raw.append(piece)
+
+        wq_passes = Wq.rearrange("(c p j) n -> c p (j n)", p=P, j=PACK)
+        wq_raw = []
+
+        def load_wq(c):
+            raw = wide_in.tile([P, PACK, UNIT], BF16, name="wq_raw")
+            nc.sync.dma_start(out=raw[:].rearrange("p j n -> p (j n)"), in_=wq_passes[c])
+            wq_raw.append(raw)
+
+        for c in range(WQ_AHEAD):
+            if c < CHUNKS:
+                load_x(c)
+            load_wq(c)
+
+        x_codes = const.tile([P, PASSES * BATCH * SEQ], U32, name="x_codes", align_bytes=64)
+        x_scales = const.tile([P, PASSES * BATCH * SEQ], U8, name="x_scales", align_bytes=64)
+
+        def transpose_x(chunk):
+            banks = []
+            for b in range(BATCH):
+                words = x_raw[chunk * BATCH + b][:].bitcast(F32).rearrange("t (g p u) -> t g u p", g=GROUP, u=2)
+                for first in range(0, GROUP, 2):
+                    bank = spare_banks.tile([P, 2, 2, SEQ], F32, name="x_bank", tag="spare")
+                    for u in range(2):
+                        for g in range(2):
+                            nc.tensor.transpose(out=bank[:, u, g, :], in_=words[:, first + g, u, :], identity=ident[:])
+                    banks.append(bank)
+            return banks
+
+        def copy_x(banks):
+            grouped = grouped_pool.tile([P, UNIT * PACK], BF16, name="x_grouped", tag="grouped", align_bytes=64)
+            grouped_words = grouped[:].bitcast(F32).rearrange("p (g b t u) -> p g b t u", g=GROUP, b=BATCH, u=2)
+            for i, bank in enumerate(banks):
+                b, first = i // 2, 2 * (i % 2)
+                copy = nc.vector.tensor_copy if i == len(banks) - 1 else nc.scalar.copy
+                copy(out=grouped_words[:, first : first + 2, b, :, :], in_=bank[:].rearrange("p u g t -> p g t u"))
+            return grouped
+
+        def quantise_x(chunk, grouped):
+            cols = slice(chunk * UNIT, (chunk + 1) * UNIT)
+            quantise(grouped[:], x_codes[:, cols], x_scales[:, cols])
+
+        q_acc = [q_banks.tile([P, BANK], F32, name="q_acc_%d" % i) for i in range(BATCH * UNIT // BANK)]
+
+        def regroup_wq(c):
+            grouped = grouped_pool.tile([P, UNIT, PACK], BF16, name="w_grouped", tag="grouped", align_bytes=64)
+            regroup(nc.vector.tensor_copy, grouped[:, : UNIT // 2, :], wq_raw[c][:, :, : UNIT // 2])
+            regroup(nc.scalar.copy, grouped[:, UNIT // 2 :, :], wq_raw[c][:, :, UNIT // 2 :])
+            if c + WQ_AHEAD < PASSES:
+                load_wq(c + WQ_AHEAD)
+            return grouped
+
+        def multiply_q(c, grouped):
+            codes, scales = quantise_weights(grouped)
+            for b in range(BATCH):
+                for half in range(UNIT // BANK):
+                    cols = slice(half * BANK, (half + 1) * BANK)
+                    multiply(q_acc[b * (UNIT // BANK) + half], c, b, codes, scales, cols)
+
+        banks = transpose_x(0)
+        for c in range(CHUNKS):
+            x_grouped = copy_x(banks)
+            if c + 1 < CHUNKS:
+                banks = transpose_x(c + 1)
+            w_grouped = regroup_wq(c)
+            quantise_x(c, x_grouped)
+            multiply_q(c, w_grouped)
+        previous = regroup_wq(CHUNKS)
+        for c in range(CHUNKS + 1, PASSES):
+            current = regroup_wq(c)
+            multiply_q(c - 1, previous)
+            previous = current
+
+        def load_head(w, unit):
+            raw = narrow_in.tile([P, GROUP, PACK, HEAD_DIM], BF16, name="head_raw", tag="narrow")
+            rows = w[unit * GROUP * K_PASS : (unit + 1) * GROUP * K_PASS, :]
+            nc.sync.dma_start(
+                out=raw[:].rearrange("p g j n -> p g (j n)"),
+                in_=rows.rearrange("(g p j) n -> p g (j n)", p=P, j=PACK),
+            )
+            return raw
+
+        k_raw, v_raw = [], []
+        for unit in range(CHUNKS):
+            k_raw.append(load_head(Wk, unit))
+            v_raw.append(load_head(Wv, unit))
+
+        k_acc = [spare_banks.tile([P, HEAD_DIM], F32, name="k_acc", tag="spare") for b in range(BATCH)]
+        v_acc = [spare_banks.tile([P, HEAD_DIM], F32, name="v_acc", tag="spare") for b in range(BATCH)]
+
+        def regroup_heads(unit):
+            grouped = grouped_pool.tile([P, UNIT, PACK], BF16, name="w_grouped", tag="grouped", align_bytes=64)
+            for g in range(GROUP):
+                k_cols = slice(g * HEAD_DIM, (g + 1) * HEAD_DIM)
+                v_cols = slice(UNIT // 2 + g * HEAD_DIM, UNIT // 2 + (g + 1) * HEAD_DIM)
+                k_copy = nc.vector.tensor_copy if g < GROUP // 2 else nc.scalar.copy
+                regroup(k_copy, grouped[:, k_cols, :], k_raw[unit][:, g, :, :])
+                regroup(nc.scalar.copy, grouped[:, v_cols, :], v_raw[unit][:, g, :, :])
+            return grouped
+
+        def multiply_heads(unit, grouped):
+            codes, scales = quantise_weights(grouped)
+            for g in range(GROUP):
+                for b in range(BATCH):
+                    k_cols = slice(g * HEAD_DIM, (g + 1) * HEAD_DIM)
+                    v_cols = slice(UNIT // 2 + g * HEAD_DIM, UNIT // 2 + (g + 1) * HEAD_DIM)
+                    multiply(k_acc[b], unit * GROUP + g, b, codes, scales, k_cols)
+                    multiply(v_acc[b], unit * GROUP + g, b, codes, scales, v_cols)
+
+        current = regroup_heads(0)
+        multiply_q(PASSES - 1, previous)
+        previous = current
+        heads_in_bank = BANK // HEAD_DIM
+        for unit in range(CHUNKS):
+            if unit + 1 < CHUNKS:
+                current = regroup_heads(unit + 1)
+            multiply_heads(unit, previous)
+            previous = current
+            b, half = divmod(unit, UNIT // BANK)
+            first_head = half * heads_in_bank
+            rope_and_store(
+                q_acc[unit],
+                heads_in_bank,
+                out_0[b, first_head : first_head + heads_in_bank].rearrange("h t d -> t h d"),
+            )
+
+        for b in range(BATCH):
+            value = rope_pool.tile([P, HEAD_DIM], F32, name="value")
+            nc.scalar.copy(out=value[:], in_=v_acc[b][:])
+            nc.sync.dma_start(out=out_2[b], in_=value[:])
+        for b in range(BATCH):
+            rope_and_store(k_acc[b], 1, out_1[b].unsqueeze(1))

@@ -26,16 +26,21 @@ BANK = 512
 UNIT = 1024
 GROUP = 4
 CHUNKS = PASSES // GROUP
+HEAD_GROUP = UNIT // HEAD_DIM
+HEAD_UNITS = PASSES // HEAD_GROUP
 RUN = 4
-WQ_AHEAD = 6
+WQ_AHEAD = 8
+VECTOR_COLS = 512
+FIRST_VECTOR_COLS = 768
+HEAD_VECTOR_COLS = 192
+HEAD_TENSOR_PASSES = 0
+X_EVERY = 3
 ROUND = 1.5 * 2.0**23
 
 FLOPS = 2 * BATCH * SEQ * EMB * (Q_HEADS + 2) * HEAD_DIM
 
 assert 2**PAIR_BITS == PAIRS
-assert GROUP * BATCH * SEQ == UNIT and GROUP * 2 * HEAD_DIM == UNIT and Q_HEADS * HEAD_DIM == UNIT
-assert BATCH * UNIT // BANK == CHUNKS
-assert CHUNKS <= WQ_AHEAD
+assert GROUP * BATCH * SEQ == UNIT and Q_HEADS * HEAD_DIM == UNIT
 
 
 def tile_groupropeattention_pa_k_kernel(tc, x, Wq, Wk, Wv, out_0, out_1, out_2):
@@ -43,53 +48,93 @@ def tile_groupropeattention_pa_k_kernel(tc, x, Wq, Wk, Wv, out_0, out_1, out_2):
     with ExitStack() as ctx:
         ctx.enter_context(tc.manual_schedule())
         const = ctx.enter_context(tc.tile_pool(name="const", bufs=1))
-        narrow_in = ctx.enter_context(tc.tile_pool(name="narrow_in", bufs=2 * CHUNKS))
+        x_in = ctx.enter_context(tc.tile_pool(name="x_in", bufs=2 * CHUNKS))
+        head_in = ctx.enter_context(tc.tile_pool(name="head_in", bufs=2 * HEAD_UNITS))
         wide_in = ctx.enter_context(tc.tile_pool(name="wide_in", bufs=WQ_AHEAD))
-        grouped_pool = ctx.enter_context(tc.tile_pool(name="grouped", bufs=3))
-        mx_pool = ctx.enter_context(tc.tile_pool(name="mx", bufs=3))
-        rope_pool = ctx.enter_context(tc.tile_pool(name="rope", bufs=2))
-        q_banks = ctx.enter_context(tc.psum_pool(name="q_banks", bufs=1))
-        spare_banks = ctx.enter_context(tc.psum_pool(name="spare_banks", bufs=4))
+        w_grouped_pool = ctx.enter_context(tc.tile_pool(name="w_grouped_pool", bufs=3))
+        x_grouped_pool = ctx.enter_context(tc.tile_pool(name="x_grouped_pool", bufs=2))
+        mx_pool = ctx.enter_context(tc.tile_pool(name="mx", bufs=5))
+        rope_pool = ctx.enter_context(tc.tile_pool(name="rope", bufs=4))
+        psum = ctx.enter_context(tc.psum_pool(name="psum", bufs=1))
 
+        x_raw = {}
+
+        def load_x(chunk, b):
+            piece = x_in.tile([P, GROUP * K_PASS], BF16, name="x_raw")
+            nc.sync.dma_start(out=piece[:], in_=x[b, :, chunk * GROUP * K_PASS : (chunk + 1) * GROUP * K_PASS])
+            x_raw[chunk, b] = piece
+
+        wq_passes = Wq.rearrange("(c p j) n -> c p j n", p=P, j=PACK)
+        wq_raw = []
+
+        def x_piece_behind(c):
+            chunk, b = c // X_EVERY, c % X_EVERY - 1
+            return (chunk, b) if chunk < CHUNKS and b >= 0 else None
+
+        def load_wq(c):
+            raw = wide_in.tile([P, PACK, UNIT], BF16, name="wq_raw")
+            parts = 2 if c in (0, PASSES - 1) else 1
+            width = UNIT // parts
+            for i in range(parts):
+                cols = slice(i * width, (i + 1) * width)
+                nc.sync.dma_start(out=raw[:, :, cols], in_=wq_passes[c][:, :, cols])
+            wq_raw.append(raw)
+            if x_piece_behind(c):
+                load_x(*x_piece_behind(c))
+
+        for c in range(WQ_AHEAD):
+            load_wq(c)
+
+        warm = const.tile([P, 1], F32, name="warm")
+        nc.vector.memset(warm[:], 0.0)
+        warm_sin = const.tile([P, 1], F32, name="warm_sin")
+        nc.scalar.activation(out=warm_sin[:], in_=warm[:], func=ACT.Sin)
         position = const.tile([P, 1], I32, name="position")
         nc.gpsimd.iota(position[:], pattern=[[0, 1]], base=0, channel_multiplier=1)
         ident = const.tile([P, P], F32, name="ident")
         make_identity(nc, ident[:])
+        ident_bf16 = const.tile([P, P], BF16, name="ident_bf16")
+        make_identity(nc, ident_bf16[:])
 
         position_turns = const.tile([P, 1], F32, name="position_turns")
-        nc.vector.tensor_scalar_mul(out=position_turns[:], in0=position[:], scalar1=1.0 / (2.0 * math.pi))
         frequency = const.tile([P, PAIRS], F32, name="frequency")
         nc.vector.memset(frequency[:], 1.0)
         for level in range(PAIR_BITS):
             bit = 2**level
             bit_set = frequency[:].rearrange("p (a two s) -> p a two s", two=2, s=bit)[:, :, 1, :]
             nc.vector.tensor_scalar_mul(out=bit_set, in0=bit_set, scalar1=THETA ** (-bit / PAIRS))
-        turns = const.tile([P, 3, PAIRS], F32, name="turns")
-        for row, shift in enumerate((0.25, 0.0, 0.5)):
-            nc.vector.tensor_scalar(
-                out=turns[:, row, :],
-                in0=frequency[:],
-                scalar1=position_turns[:, 0:1],
-                scalar2=shift,
-                op0=ALU.mult,
-                op1=ALU.add,
-            )
-        whole_turns = const.tile([P, 3, PAIRS], F32, name="whole_turns")
-        nc.vector.tensor_scalar(
-            out=whole_turns[:], in0=turns[:], scalar1=ROUND, scalar2=ROUND, op0=ALU.add, op1=ALU.subtract
-        )
-        nc.vector.tensor_tensor(out=turns[:], in0=turns[:], in1=whole_turns[:], op=ALU.subtract)
+        nc.vector.tensor_scalar_mul(out=position_turns[:], in0=position[:], scalar1=1.0 / (2.0 * math.pi))
         trig = const.tile([P, 3, PAIRS], F32, name="trig")
-        nc.scalar.activation(out=trig[:], in_=turns[:], func=ACT.Sin, scale=2.0 * math.pi)
         cos, sin, minus_sin = trig[:, 0, :], trig[:, 1, :], trig[:, 2, :]
+
+        def make_trig():
+            turns = const.tile([P, 3, PAIRS], F32, name="turns")
+            for row, shift in enumerate((0.25, 0.0, 0.5)):
+                nc.vector.tensor_scalar(
+                    out=turns[:, row, :],
+                    in0=frequency[:],
+                    scalar1=position_turns[:, 0:1],
+                    scalar2=shift,
+                    op0=ALU.mult,
+                    op1=ALU.add,
+                )
+            whole_turns = const.tile([P, 3, PAIRS], F32, name="whole_turns")
+            nc.vector.tensor_scalar(
+                out=whole_turns[:], in0=turns[:], scalar1=ROUND, scalar2=ROUND, op0=ALU.add, op1=ALU.subtract
+            )
+            nc.vector.tensor_tensor(out=turns[:], in0=turns[:], in1=whole_turns[:], op=ALU.subtract)
+            nc.scalar.activation(out=trig[:], in_=turns[:], func=ACT.Sin, scale=2.0 * math.pi)
 
         def quantise(grouped, codes, scales):
             nc.vector.quantize_mx(out=codes.bitcast(FP8X4), scales=scales, in_=grouped)
 
-        def quantise_weights(grouped):
+        def quantise_weights(grouped, parts):
             codes = mx_pool.tile([P, UNIT], U32, name="w_codes", align_bytes=64)
             scales = mx_pool.tile([P, UNIT], U8, name="w_scales", align_bytes=64)
-            quantise(grouped[:].rearrange("p n j -> p (n j)"), codes[:], scales[:])
+            width = UNIT // parts
+            for i in range(parts):
+                cols = slice(i * width, (i + 1) * width)
+                quantise(grouped[:, cols, :].rearrange("p n j -> p (n j)"), codes[:, cols], scales[:, cols])
             return codes, scales
 
         def regroup(copy, grouped_cols, raw_cols):
@@ -137,142 +182,156 @@ def tile_groupropeattention_pa_k_kernel(tc, x, Wq, Wk, Wv, out_0, out_1, out_2):
             )
             nc.sync.dma_start(out=out_rows, in_=direct[:].rearrange("p h k two -> p h (k two)"))
 
-        x_raw = []
-
-        def load_x(chunk):
-            for b in range(BATCH):
-                piece = narrow_in.tile([P, GROUP * K_PASS], BF16, name="x_raw", tag="narrow")
-                nc.sync.dma_start(out=piece[:], in_=x[b, :, chunk * GROUP * K_PASS : (chunk + 1) * GROUP * K_PASS])
-                x_raw.append(piece)
-
-        wq_passes = Wq.rearrange("(c p j) n -> c p (j n)", p=P, j=PACK)
-        wq_raw = []
-
-        def load_wq(c):
-            raw = wide_in.tile([P, PACK, UNIT], BF16, name="wq_raw")
-            nc.sync.dma_start(out=raw[:].rearrange("p j n -> p (j n)"), in_=wq_passes[c])
-            wq_raw.append(raw)
-
-        for c in range(WQ_AHEAD):
-            if c < CHUNKS:
-                load_x(c)
-            load_wq(c)
-
         x_codes = const.tile([P, PASSES * BATCH * SEQ], U32, name="x_codes", align_bytes=64)
         x_scales = const.tile([P, PASSES * BATCH * SEQ], U8, name="x_scales", align_bytes=64)
+        x_grouped = {}
 
-        def transpose_x(chunk):
-            banks = []
-            for b in range(BATCH):
-                words = x_raw[chunk * BATCH + b][:].bitcast(F32).rearrange("t (g p u) -> t g u p", g=GROUP, u=2)
-                for first in range(0, GROUP, 2):
-                    bank = spare_banks.tile([P, 2, 2, SEQ], F32, name="x_bank", tag="spare")
-                    for u in range(2):
-                        for g in range(2):
-                            nc.tensor.transpose(out=bank[:, u, g, :], in_=words[:, first + g, u, :], identity=ident[:])
-                    banks.append(bank)
-            return banks
+        x_banks = {}
 
-        def copy_x(banks):
-            grouped = grouped_pool.tile([P, UNIT * PACK], BF16, name="x_grouped", tag="grouped", align_bytes=64)
-            grouped_words = grouped[:].bitcast(F32).rearrange("p (g b t u) -> p g b t u", g=GROUP, b=BATCH, u=2)
-            for i, bank in enumerate(banks):
-                b, first = i // 2, 2 * (i % 2)
-                copy = nc.vector.tensor_copy if i == len(banks) - 1 else nc.scalar.copy
-                copy(out=grouped_words[:, first : first + 2, b, :, :], in_=bank[:].rearrange("p u g t -> p g t u"))
-            return grouped
+        def transpose_x(chunk, b):
+            words = x_raw[chunk, b][:].bitcast(F32).rearrange("t (g p u) -> t g u p", g=GROUP, u=2)
+            for first in range(0, GROUP, 2):
+                bank = psum.tile([P, 2, 2, SEQ], F32, name="x_bank", tag="bank_%d" % (4 + 2 * b + first // 2))
+                for u in range(2):
+                    for g in range(2):
+                        nc.tensor.transpose(out=bank[:, u, g, :], in_=words[:, first + g, u, :], identity=ident[:])
+                x_banks[chunk, b, first] = bank
 
-        def quantise_x(chunk, grouped):
+        def copy_x(chunk, b):
+            if b == 0:
+                x_grouped[chunk] = x_grouped_pool.tile([P, UNIT * PACK], BF16, name="x_grouped", align_bytes=64)
+            grouped = x_grouped[chunk][:].bitcast(F32).rearrange("p (g b t u) -> p g b t u", g=GROUP, b=BATCH, u=2)
+            for first in range(0, GROUP, 2):
+                bank = x_banks[chunk, b, first]
+                nc.scalar.copy(out=grouped[:, first : first + 2, b, :, :], in_=bank[:].rearrange("p u g t -> p g t u"))
+
+        def quantise_x(chunk):
             cols = slice(chunk * UNIT, (chunk + 1) * UNIT)
-            quantise(grouped[:], x_codes[:, cols], x_scales[:, cols])
+            quantise(x_grouped[chunk][:], x_codes[:, cols], x_scales[:, cols])
 
-        q_acc = [q_banks.tile([P, BANK], F32, name="q_acc_%d" % i) for i in range(BATCH * UNIT // BANK)]
+        q_acc = [psum.tile([P, BANK], F32, name="q_acc", tag="bank_%d" % i) for i in range(BATCH * UNIT // BANK)]
 
         def regroup_wq(c):
-            grouped = grouped_pool.tile([P, UNIT, PACK], BF16, name="w_grouped", tag="grouped", align_bytes=64)
-            regroup(nc.vector.tensor_copy, grouped[:, : UNIT // 2, :], wq_raw[c][:, :, : UNIT // 2])
-            regroup(nc.scalar.copy, grouped[:, UNIT // 2 :, :], wq_raw[c][:, :, UNIT // 2 :])
+            grouped = w_grouped_pool.tile([P, UNIT, PACK], BF16, name="w_grouped", align_bytes=64)
+            parts = 2 if c in (0, PASSES - 1) else 1
+            width = UNIT // parts
+            mine = (FIRST_VECTOR_COLS if c == 0 else VECTOR_COLS) // parts
+            for i in range(parts):
+                a, b, e = i * width, i * width + mine, (i + 1) * width
+                regroup(nc.vector.tensor_copy, grouped[:, a:b, :], wq_raw[c][:, :, a:b])
+                regroup(nc.scalar.copy, grouped[:, b:e, :], wq_raw[c][:, :, b:e])
             if c + WQ_AHEAD < PASSES:
                 load_wq(c + WQ_AHEAD)
             return grouped
 
-        def multiply_q(c, grouped):
-            codes, scales = quantise_weights(grouped)
-            for b in range(BATCH):
-                for half in range(UNIT // BANK):
-                    cols = slice(half * BANK, (half + 1) * BANK)
-                    multiply(q_acc[b * (UNIT // BANK) + half], c, b, codes, scales, cols)
+        quantised = {}
 
-        banks = transpose_x(0)
-        for c in range(CHUNKS):
-            x_grouped = copy_x(banks)
-            if c + 1 < CHUNKS:
-                banks = transpose_x(c + 1)
-            w_grouped = regroup_wq(c)
-            quantise_x(c, x_grouped)
-            multiply_q(c, w_grouped)
-        previous = regroup_wq(CHUNKS)
-        for c in range(CHUNKS + 1, PASSES):
-            current = regroup_wq(c)
-            multiply_q(c - 1, previous)
-            previous = current
+        def multiply_q(c):
+            for half in range(UNIT // BANK):
+                for b in range(BATCH):
+                    cols = slice(half * BANK, (half + 1) * BANK)
+                    multiply(q_acc[half * BATCH + b], c, b, *quantised[c], cols)
+
+        grouped = {}
+        multiplied = 0
+        for c in range(PASSES):
+            grouped[c] = regroup_wq(c)
+            piece = x_piece_behind(c)
+            if piece:
+                copy_x(*piece)
+            if c + 1 < PASSES and x_piece_behind(c + 1):
+                transpose_x(*x_piece_behind(c + 1))
+            if c == 0:
+                continue
+            if c == 1:
+                make_trig()
+            quantised[c - 1] = quantise_weights(grouped[c - 1], 1)
+            done = x_piece_behind(c - 1)
+            if done and done[1] == BATCH - 1:
+                quantise_x(done[0])
+                x_ready = (done[0] + 1) * GROUP
+            for turn in range(2):
+                if c >= X_EVERY and multiplied < min(c, x_ready):
+                    multiply_q(multiplied)
+                    multiplied += 1
 
         def load_head(w, unit):
-            raw = narrow_in.tile([P, GROUP, PACK, HEAD_DIM], BF16, name="head_raw", tag="narrow")
-            rows = w[unit * GROUP * K_PASS : (unit + 1) * GROUP * K_PASS, :]
+            raw = head_in.tile([P, HEAD_GROUP, PACK, HEAD_DIM], BF16, name="head_raw")
+            rows = w[unit * HEAD_GROUP * K_PASS : (unit + 1) * HEAD_GROUP * K_PASS, :]
             nc.sync.dma_start(
                 out=raw[:].rearrange("p g j n -> p g (j n)"),
                 in_=rows.rearrange("(g p j) n -> p g (j n)", p=P, j=PACK),
             )
             return raw
 
-        k_raw, v_raw = [], []
-        for unit in range(CHUNKS):
-            k_raw.append(load_head(Wk, unit))
-            v_raw.append(load_head(Wv, unit))
+        head_raw = [load_head(w, unit) for w in (Wk, Wv) for unit in range(HEAD_UNITS)]
+        k_acc = [psum.tile([P, HEAD_DIM], F32, name="k_acc", tag="bank_%d" % (4 + b)) for b in range(BATCH)]
+        v_acc = []
 
-        k_acc = [spare_banks.tile([P, HEAD_DIM], F32, name="k_acc", tag="spare") for b in range(BATCH)]
-        v_acc = [spare_banks.tile([P, HEAD_DIM], F32, name="v_acc", tag="spare") for b in range(BATCH)]
-
-        def regroup_heads(unit):
-            grouped = grouped_pool.tile([P, UNIT, PACK], BF16, name="w_grouped", tag="grouped", align_bytes=64)
-            for g in range(GROUP):
-                k_cols = slice(g * HEAD_DIM, (g + 1) * HEAD_DIM)
-                v_cols = slice(UNIT // 2 + g * HEAD_DIM, UNIT // 2 + (g + 1) * HEAD_DIM)
-                k_copy = nc.vector.tensor_copy if g < GROUP // 2 else nc.scalar.copy
-                regroup(k_copy, grouped[:, k_cols, :], k_raw[unit][:, g, :, :])
-                regroup(nc.scalar.copy, grouped[:, v_cols, :], v_raw[unit][:, g, :, :])
+        def regroup_head(i):
+            grouped = w_grouped_pool.tile([P, UNIT, PACK], BF16, name="w_grouped", align_bytes=64)
+            for g in range(HEAD_GROUP):
+                mine = min(max(HEAD_VECTOR_COLS - g * HEAD_DIM, 0), HEAD_DIM)
+                a, b, e = g * HEAD_DIM, g * HEAD_DIM + mine, (g + 1) * HEAD_DIM
+                if b > a:
+                    regroup(nc.vector.tensor_copy, grouped[:, a:b, :], head_raw[i][:, g, :, :mine])
+                if e > b and g < HEAD_GROUP - HEAD_TENSOR_PASSES:
+                    regroup(nc.scalar.copy, grouped[:, b:e, :], head_raw[i][:, g, :, mine:])
+            g = HEAD_GROUP - HEAD_TENSOR_PASSES
+            while g < HEAD_GROUP:
+                count = min(2, HEAD_GROUP - g)
+                stage = psum.tile([P, 2, HEAD_DIM, PACK], BF16, name="stage", tag="bank_%d" % (6 + len(stages) % 2))
+                stages.append(stage)
+                for k in range(count):
+                    nc.tensor.matmul(
+                        out=stage[:, k, :, :],
+                        lhsT=ident_bf16[:],
+                        rhs=head_raw[i][:, g + k, :, :].rearrange("p j n -> p n j"),
+                        start=True,
+                        stop=True,
+                    )
+                nc.scalar.copy(
+                    out=grouped[:, g * HEAD_DIM : (g + count) * HEAD_DIM, :].rearrange("p n j -> p (n j)"),
+                    in_=stage[:, :count, :, :].rearrange("p k n j -> p (k n j)"),
+                )
+                g += count
             return grouped
 
-        def multiply_heads(unit, grouped):
-            codes, scales = quantise_weights(grouped)
-            for g in range(GROUP):
-                for b in range(BATCH):
-                    k_cols = slice(g * HEAD_DIM, (g + 1) * HEAD_DIM)
-                    v_cols = slice(UNIT // 2 + g * HEAD_DIM, UNIT // 2 + (g + 1) * HEAD_DIM)
-                    multiply(k_acc[b], unit * GROUP + g, b, codes, scales, k_cols)
-                    multiply(v_acc[b], unit * GROUP + g, b, codes, scales, v_cols)
+        stages = []
 
-        current = regroup_heads(0)
-        multiply_q(PASSES - 1, previous)
-        previous = current
+        def multiply_head(i, codes, scales):
+            acc = k_acc if i < HEAD_UNITS else v_acc
+            for g in range(HEAD_GROUP):
+                for b in range(BATCH):
+                    cols = slice(g * HEAD_DIM, (g + 1) * HEAD_DIM)
+                    multiply(acc[b], i % HEAD_UNITS * HEAD_GROUP + g, b, codes, scales, cols)
+
         heads_in_bank = BANK // HEAD_DIM
-        for unit in range(CHUNKS):
-            if unit + 1 < CHUNKS:
-                current = regroup_heads(unit + 1)
-            multiply_heads(unit, previous)
-            previous = current
-            b, half = divmod(unit, UNIT // BANK)
-            first_head = half * heads_in_bank
-            rope_and_store(
-                q_acc[unit],
-                heads_in_bank,
-                out_0[b, first_head : first_head + heads_in_bank].rearrange("h t d -> t h d"),
-            )
+
+        def rope_q(i):
+            half, b = divmod(i, BATCH)
+            heads = slice(half * heads_in_bank, (half + 1) * heads_in_bank)
+            rope_and_store(q_acc[i], heads_in_bank, out_0[b, heads].rearrange("h t d -> t h d"))
+
+        head_grouped = [regroup_head(0)]
+        quantised[PASSES - 1] = quantise_weights(grouped[PASSES - 1], 2)
+        multiply_q(PASSES - 1)
+        head_grouped.append(regroup_head(1))
+        rope_q(0)
+        multiply_head(0, *quantise_weights(head_grouped[0], 1))
+        rope_q(1)
+        head_grouped.append(regroup_head(2))
+        multiply_head(1, *quantise_weights(head_grouped[1], 1))
+        rope_q(2)
+        head_grouped.append(regroup_head(3))
+        v_acc.extend([psum.tile([P, HEAD_DIM], F32, name="v_acc", tag="bank_%d" % b) for b in range(BATCH)])
+        multiply_head(2, *quantise_weights(head_grouped[2], 1))
+        for b in range(BATCH):
+            rope_and_store(k_acc[b], 1, out_1[b].unsqueeze(1))
+        multiply_head(3, *quantise_weights(head_grouped[3], 1))
+        rope_q(3)
 
         for b in range(BATCH):
             value = rope_pool.tile([P, HEAD_DIM], F32, name="value")
             nc.scalar.copy(out=value[:], in_=v_acc[b][:])
             nc.sync.dma_start(out=out_2[b], in_=value[:])
-        for b in range(BATCH):
-            rope_and_store(k_acc[b], 1, out_1[b].unsqueeze(1))

@@ -31,7 +31,6 @@ HEAD_UNITS = PASSES // HEAD_GROUP
 RUN = 4
 WQ_AHEAD = 8
 VECTOR_COLS = 512
-FIRST_VECTOR_COLS = 768
 HEAD_VECTOR_COLS = 192
 HEAD_TENSOR_PASSES = 0
 X_EVERY = 3
@@ -64,7 +63,7 @@ def tile_groupropeattention_pa_k_kernel(tc, x, Wq, Wk, Wv, out_0, out_1, out_2):
             nc.sync.dma_start(out=piece[:], in_=x[b, :, chunk * GROUP * K_PASS : (chunk + 1) * GROUP * K_PASS])
             x_raw[chunk, b] = piece
 
-        wq_passes = Wq.rearrange("(c p j) n -> c p j n", p=P, j=PACK)
+        wq_passes = Wq.rearrange("(c p j) n -> c p (j n)", p=P, j=PACK)
         wq_raw = []
 
         def x_piece_behind(c):
@@ -73,11 +72,7 @@ def tile_groupropeattention_pa_k_kernel(tc, x, Wq, Wk, Wv, out_0, out_1, out_2):
 
         def load_wq(c):
             raw = wide_in.tile([P, PACK, UNIT], BF16, name="wq_raw")
-            parts = 2 if c in (0, PASSES - 1) else 1
-            width = UNIT // parts
-            for i in range(parts):
-                cols = slice(i * width, (i + 1) * width)
-                nc.sync.dma_start(out=raw[:, :, cols], in_=wq_passes[c][:, :, cols])
+            nc.sync.dma_start(out=raw[:].rearrange("p j n -> p (j n)"), in_=wq_passes[c])
             wq_raw.append(raw)
             if x_piece_behind(c):
                 load_x(*x_piece_behind(c))
@@ -213,13 +208,8 @@ def tile_groupropeattention_pa_k_kernel(tc, x, Wq, Wk, Wv, out_0, out_1, out_2):
 
         def regroup_wq(c):
             grouped = w_grouped_pool.tile([P, UNIT, PACK], BF16, name="w_grouped", align_bytes=64)
-            parts = 2 if c in (0, PASSES - 1) else 1
-            width = UNIT // parts
-            mine = (FIRST_VECTOR_COLS if c == 0 else VECTOR_COLS) // parts
-            for i in range(parts):
-                a, b, e = i * width, i * width + mine, (i + 1) * width
-                regroup(nc.vector.tensor_copy, grouped[:, a:b, :], wq_raw[c][:, :, a:b])
-                regroup(nc.scalar.copy, grouped[:, b:e, :], wq_raw[c][:, :, b:e])
+            regroup(nc.vector.tensor_copy, grouped[:, :VECTOR_COLS, :], wq_raw[c][:, :, :VECTOR_COLS])
+            regroup(nc.scalar.copy, grouped[:, VECTOR_COLS:, :], wq_raw[c][:, :, VECTOR_COLS:])
             if c + WQ_AHEAD < PASSES:
                 load_wq(c + WQ_AHEAD)
             return grouped

@@ -26,14 +26,22 @@ BANK = 512
 UNIT = 1024
 GROUP = 4
 CHUNKS = PASSES // GROUP
-HEAD_GROUP = UNIT // HEAD_DIM
-HEAD_UNITS = PASSES // HEAD_GROUP
+HEADS = (
+    (0, 0, 8, 0, 0),
+    (0, 8, 8, 0, 4),
+    (1, 0, 8, 0, 4),
+    (1, 8, 4, 128, 2),
+    (1, 12, 4, 128, 2),
+)
 RUN = 4
-WQ_AHEAD = 8
+WQ_AHEAD = 6
 VECTOR_COLS = 512
-HEAD_VECTOR_COLS = 192
-HEAD_TENSOR_PASSES = 0
+LAST_VECTOR_COLS = 512
+FIRST_TENSOR_PASS = 12
+LATE_VECTOR_COLS = 384
+TENSOR_COLS = 128
 X_EVERY = 3
+STAGE_BANKS = (6, 7, 2, 3)
 ROUND = 1.5 * 2.0**23
 
 FLOPS = 2 * BATCH * SEQ * EMB * (Q_HEADS + 2) * HEAD_DIM
@@ -48,9 +56,9 @@ def tile_groupropeattention_pa_k_kernel(tc, x, Wq, Wk, Wv, out_0, out_1, out_2):
         ctx.enter_context(tc.manual_schedule())
         const = ctx.enter_context(tc.tile_pool(name="const", bufs=1))
         x_in = ctx.enter_context(tc.tile_pool(name="x_in", bufs=2 * CHUNKS))
-        head_in = ctx.enter_context(tc.tile_pool(name="head_in", bufs=2 * HEAD_UNITS))
+        head_in = ctx.enter_context(tc.tile_pool(name="head_in", bufs=1))
         wide_in = ctx.enter_context(tc.tile_pool(name="wide_in", bufs=WQ_AHEAD))
-        w_grouped_pool = ctx.enter_context(tc.tile_pool(name="w_grouped_pool", bufs=3))
+        w_grouped_pool = ctx.enter_context(tc.tile_pool(name="w_grouped_pool", bufs=5))
         x_grouped_pool = ctx.enter_context(tc.tile_pool(name="x_grouped_pool", bufs=2))
         mx_pool = ctx.enter_context(tc.tile_pool(name="mx", bufs=5))
         rope_pool = ctx.enter_context(tc.tile_pool(name="rope", bufs=4))
@@ -150,7 +158,7 @@ def tile_groupropeattention_pa_k_kernel(tc, x, Wq, Wk, Wv, out_0, out_1, out_2):
                 stop=(c == PASSES - 1),
             )
 
-        def rope_and_store(acc, heads, out_rows):
+        def rope_products(acc, heads):
             pairs = acc[:].rearrange("p (h k two) -> p h k two", h=heads, two=2)
             direct = rope_pool.tile([P, heads, PAIRS, 2], F32, name="direct")
             nc.vector.tensor_tensor(
@@ -172,7 +180,11 @@ def tile_groupropeattention_pa_k_kernel(tc, x, Wq, Wk, Wv, out_0, out_1, out_2):
                 in1=sin.unsqueeze(1).to_broadcast([P, heads, PAIRS]),
                 op=ALU.mult,
             )
-            nc.vector.tensor_tensor(
+            return direct, crossed
+
+        def rope_sum(engine, products, out_rows):
+            direct, crossed = products
+            engine.tensor_tensor(
                 out=direct[:], in0=direct[:], in1=crossed[:].rearrange("p h two k -> p h k two"), op=ALU.add
             )
             nc.sync.dma_start(out=out_rows, in_=direct[:].rearrange("p h k two -> p h (k two)"))
@@ -206,10 +218,44 @@ def tile_groupropeattention_pa_k_kernel(tc, x, Wq, Wk, Wv, out_0, out_1, out_2):
 
         q_acc = [psum.tile([P, BANK], F32, name="q_acc", tag="bank_%d" % i) for i in range(BATCH * UNIT // BANK)]
 
+        stages = []
+
+        def regroup_by_tensor(pieces, bank):
+            stage = psum.tile([P, len(pieces), HEAD_DIM, PACK], BF16, name="stage", tag="bank_%d" % bank)
+            stages.append(stage)
+            for k, raw in enumerate(pieces):
+                nc.tensor.matmul(
+                    out=stage[:, k, :, :], lhsT=ident_bf16[:], rhs=raw.rearrange("p j n -> p n j"), start=True, stop=True
+                )
+            return stage
+
+        def empty_stage(stage, grouped_cols):
+            nc.scalar.copy(
+                out=grouped_cols.rearrange("p n j -> p (n j)"), in_=stage[:].rearrange("p k n j -> p (k n j)")
+            )
+
+        wq_stages = {}
+
+        def stage_wq(c):
+            if FIRST_TENSOR_PASS <= c < PASSES - 1:
+                starts = range(UNIT - TENSOR_COLS, UNIT, HEAD_DIM)
+                wq_stages[c] = regroup_by_tensor([wq_raw[c][:, :, i : i + HEAD_DIM] for i in starts], 6 + c % 2)
+
         def regroup_wq(c):
             grouped = w_grouped_pool.tile([P, UNIT, PACK], BF16, name="w_grouped", align_bytes=64)
-            regroup(nc.vector.tensor_copy, grouped[:, :VECTOR_COLS, :], wq_raw[c][:, :, :VECTOR_COLS])
-            regroup(nc.scalar.copy, grouped[:, VECTOR_COLS:, :], wq_raw[c][:, :, VECTOR_COLS:])
+            raw = wq_raw[c]
+            if c < PASSES - 1:
+                helped = c >= FIRST_TENSOR_PASS
+                a, b = (LATE_VECTOR_COLS, UNIT - TENSOR_COLS) if helped else (VECTOR_COLS, UNIT)
+                regroup(nc.vector.tensor_copy, grouped[:, :a, :], raw[:, :, :a])
+                regroup(nc.scalar.copy, grouped[:, a:b, :], raw[:, :, a:b])
+                if helped:
+                    empty_stage(wq_stages[c], grouped[:, b:, :])
+            else:
+                for first in range(0, UNIT, UNIT // 2):
+                    a, b = first + LAST_VECTOR_COLS // 2, first + UNIT // 2
+                    regroup(nc.vector.tensor_copy, grouped[:, first:a, :], raw[:, :, first:a])
+                    regroup(nc.scalar.copy, grouped[:, a:b, :], raw[:, :, a:b])
             if c + WQ_AHEAD < PASSES:
                 load_wq(c + WQ_AHEAD)
             return grouped
@@ -225,17 +271,21 @@ def tile_groupropeattention_pa_k_kernel(tc, x, Wq, Wk, Wv, out_0, out_1, out_2):
         grouped = {}
         multiplied = 0
         for c in range(PASSES):
+            if c == PASSES - 1:
+                quantised[c - 1] = quantise_weights(grouped[c - 1], 1)
             grouped[c] = regroup_wq(c)
             piece = x_piece_behind(c)
             if piece:
                 copy_x(*piece)
             if c + 1 < PASSES and x_piece_behind(c + 1):
                 transpose_x(*x_piece_behind(c + 1))
+            stage_wq(c + 1)
             if c == 0:
                 continue
             if c == 1:
                 make_trig()
-            quantised[c - 1] = quantise_weights(grouped[c - 1], 1)
+            if c < PASSES - 1:
+                quantised[c - 1] = quantise_weights(grouped[c - 1], 1)
             done = x_piece_behind(c - 1)
             if done and done[1] == BATCH - 1:
                 quantise_x(done[0])
@@ -245,81 +295,96 @@ def tile_groupropeattention_pa_k_kernel(tc, x, Wq, Wk, Wv, out_0, out_1, out_2):
                     multiply_q(multiplied)
                     multiplied += 1
 
-        def load_head(w, unit):
-            raw = head_in.tile([P, HEAD_GROUP, PACK, HEAD_DIM], BF16, name="head_raw")
-            rows = w[unit * HEAD_GROUP * K_PASS : (unit + 1) * HEAD_GROUP * K_PASS, :]
+        head_raw = []
+        for i, (matrix, first, count, mine, by_tensor) in enumerate(HEADS):
+            raw = head_in.tile([P, count, PACK, HEAD_DIM], BF16, name="head_raw", tag="head_raw_%d" % i)
+            rows = (Wk, Wv)[matrix][first * K_PASS : (first + count) * K_PASS, :]
             nc.sync.dma_start(
                 out=raw[:].rearrange("p g j n -> p g (j n)"),
                 in_=rows.rearrange("(g p j) n -> p g (j n)", p=P, j=PACK),
             )
-            return raw
-
-        head_raw = [load_head(w, unit) for w in (Wk, Wv) for unit in range(HEAD_UNITS)]
+            head_raw.append(raw)
         k_acc = [psum.tile([P, HEAD_DIM], F32, name="k_acc", tag="bank_%d" % (4 + b)) for b in range(BATCH)]
         v_acc = []
 
+        head_stages = {}
+
+        def stage_bank():
+            used.append(0)
+            return STAGE_BANKS[(len(used) - 1) % len(STAGE_BANKS)]
+
+        used = []
+
+        def stage_head(i):
+            matrix, first, count, mine, by_tensor = HEADS[i]
+            head_stages[i] = [
+                regroup_by_tensor([head_raw[i][:, g + k, :, :] for k in range(2)], stage_bank()) for g in range(count - by_tensor, count, 2)
+            ]
+
         def regroup_head(i):
+            matrix, first, count, mine, by_tensor = HEADS[i]
             grouped = w_grouped_pool.tile([P, UNIT, PACK], BF16, name="w_grouped", align_bytes=64)
-            for g in range(HEAD_GROUP):
-                mine = min(max(HEAD_VECTOR_COLS - g * HEAD_DIM, 0), HEAD_DIM)
-                a, b, e = g * HEAD_DIM, g * HEAD_DIM + mine, (g + 1) * HEAD_DIM
-                if b > a:
-                    regroup(nc.vector.tensor_copy, grouped[:, a:b, :], head_raw[i][:, g, :, :mine])
-                if e > b and g < HEAD_GROUP - HEAD_TENSOR_PASSES:
-                    regroup(nc.scalar.copy, grouped[:, b:e, :], head_raw[i][:, g, :, mine:])
-            g = HEAD_GROUP - HEAD_TENSOR_PASSES
-            while g < HEAD_GROUP:
-                count = min(2, HEAD_GROUP - g)
-                stage = psum.tile([P, 2, HEAD_DIM, PACK], BF16, name="stage", tag="bank_%d" % (6 + len(stages) % 2))
-                stages.append(stage)
-                for k in range(count):
-                    nc.tensor.matmul(
-                        out=stage[:, k, :, :],
-                        lhsT=ident_bf16[:],
-                        rhs=head_raw[i][:, g + k, :, :].rearrange("p j n -> p n j"),
-                        start=True,
-                        stop=True,
-                    )
-                nc.scalar.copy(
-                    out=grouped[:, g * HEAD_DIM : (g + count) * HEAD_DIM, :].rearrange("p n j -> p (n j)"),
-                    in_=stage[:, :count, :, :].rearrange("p k n j -> p (k n j)"),
-                )
-                g += count
+            for g in range(count - by_tensor):
+                cols = slice(g * HEAD_DIM, (g + 1) * HEAD_DIM)
+                copy = nc.vector.tensor_copy if g * HEAD_DIM < mine else nc.scalar.copy
+                regroup(copy, grouped[:, cols, :], head_raw[i][:, g, :, :])
+            for k, stage in enumerate(head_stages[i]):
+                g = count - by_tensor + 2 * k
+                empty_stage(stage, grouped[:, g * HEAD_DIM : (g + 2) * HEAD_DIM, :])
             return grouped
 
-        stages = []
+        def quantise_head(i, grouped):
+            width = HEADS[i][2] * HEAD_DIM
+            codes = mx_pool.tile([P, UNIT], U32, name="w_codes", align_bytes=64)
+            scales = mx_pool.tile([P, UNIT], U8, name="w_scales", align_bytes=64)
+            quantise(grouped[:, :width, :].rearrange("p n j -> p (n j)"), codes[:, :width], scales[:, :width])
+            return codes, scales
 
         def multiply_head(i, codes, scales):
-            acc = k_acc if i < HEAD_UNITS else v_acc
-            for g in range(HEAD_GROUP):
+            matrix, first, count, mine, by_tensor = HEADS[i]
+            for g in range(count):
                 for b in range(BATCH):
                     cols = slice(g * HEAD_DIM, (g + 1) * HEAD_DIM)
-                    multiply(acc[b], i % HEAD_UNITS * HEAD_GROUP + g, b, codes, scales, cols)
+                    multiply((k_acc, v_acc)[matrix][b], first + g, b, codes, scales, cols)
 
         heads_in_bank = BANK // HEAD_DIM
+
+        rope_q_out = {}
 
         def rope_q(i):
             half, b = divmod(i, BATCH)
             heads = slice(half * heads_in_bank, (half + 1) * heads_in_bank)
-            rope_and_store(q_acc[i], heads_in_bank, out_0[b, heads].rearrange("h t d -> t h d"))
+            rope_q_out[i] = (rope_products(q_acc[i], heads_in_bank), out_0[b, heads].rearrange("h t d -> t h d"))
 
-        head_grouped = [regroup_head(0)]
+        head_grouped = {}
+
+        def rg(i):
+            head_grouped[i] = regroup_head(i)
+
+        def qm(i):
+            multiply_head(i, *quantise_head(i, head_grouped[i]))
+
         quantised[PASSES - 1] = quantise_weights(grouped[PASSES - 1], 2)
         multiply_q(PASSES - 1)
-        head_grouped.append(regroup_head(1))
-        rope_q(0)
-        multiply_head(0, *quantise_weights(head_grouped[0], 1))
-        rope_q(1)
-        head_grouped.append(regroup_head(2))
-        multiply_head(1, *quantise_weights(head_grouped[1], 1))
-        rope_q(2)
-        head_grouped.append(regroup_head(3))
+        stage_head(0)
+        rg(0)
+        for i in range(BATCH * UNIT // BANK):
+            rope_q(i)
+            if i:
+                rope_sum(nc.vector, *rope_q_out[i - 1])
+        rope_sum(nc.vector, *rope_q_out[i])
+        for i in range(1, len(HEADS)):
+            stage_head(i)
+            rg(i)
         v_acc.extend([psum.tile([P, HEAD_DIM], F32, name="v_acc", tag="bank_%d" % b) for b in range(BATCH)])
-        multiply_head(2, *quantise_weights(head_grouped[2], 1))
+        qm(0)
+        qm(1)
+        qm(2)
+        qm(3)
+        rope_k = [rope_products(k_acc[b], 1) for b in range(BATCH)]
         for b in range(BATCH):
-            rope_and_store(k_acc[b], 1, out_1[b].unsqueeze(1))
-        multiply_head(3, *quantise_weights(head_grouped[3], 1))
-        rope_q(3)
+            rope_sum(nc.vector, rope_k[b], out_1[b].unsqueeze(1))
+        qm(4)
 
         for b in range(BATCH):
             value = rope_pool.tile([P, HEAD_DIM], F32, name="value")

@@ -225,7 +225,7 @@ def tile_groupropeattention_pa_k_kernel(tc, x, Wq, Wk, Wv, out_0, out_1, out_2):
             stages.append(stage)
             for k, raw in enumerate(pieces):
                 nc.tensor.matmul(
-                    out=stage[:, k, :, :], lhsT=ident_bf16[:], rhs=raw.rearrange("p j n -> p n j"), start=True, stop=True
+                    out=stage[:, k, :, :].rearrange("p n j -> p j n"), lhsT=ident_bf16[:], rhs=raw, start=True, stop=True
                 )
             return stage
 

@@ -35,13 +35,14 @@ HEADS = (
 )
 RUN = 4
 WQ_AHEAD = 6
-VECTOR_COLS = 512
+VECTOR_COLS = 544
 LAST_VECTOR_COLS = 512
 FIRST_TENSOR_PASS = 12
-LATE_VECTOR_COLS = 384
-TENSOR_COLS = 128
+LATE_VECTOR_COLS = 448
+TENSOR_COLS = 256
 X_EVERY = 3
-STAGE_BANKS = (6, 7, 2, 3)
+STAGE_BANKS = (6, 7, 0, 1)
+K0_AFTER = 1
 ROUND = 1.5 * 2.0**23
 
 FLOPS = 2 * BATCH * SEQ * EMB * (Q_HEADS + 2) * HEAD_DIM
@@ -321,13 +322,20 @@ def tile_groupropeattention_pa_k_kernel(tc, x, Wq, Wk, Wv, out_0, out_1, out_2):
                 regroup_by_tensor([head_raw[i][:, g + k, :, :] for k in range(2)], stage_bank()) for g in range(count - by_tensor, count, 2)
             ]
 
+        def regroup_passes(copy, grouped, raw, first, end):
+            copy(
+                out=grouped[:, first * HEAD_DIM : end * HEAD_DIM, :].rearrange("p (g c i) j -> p g c j i", c=HEAD_DIM // RUN, i=RUN),
+                in_=raw[:, first:end, :, :].rearrange("p g j (c i) -> p g c j i", i=RUN),
+            )
+
         def regroup_head(i):
             matrix, first, count, mine, by_tensor = HEADS[i]
             grouped = w_grouped_pool.tile([P, UNIT, PACK], BF16, name="w_grouped", align_bytes=64)
-            for g in range(count - by_tensor):
-                cols = slice(g * HEAD_DIM, (g + 1) * HEAD_DIM)
-                copy = nc.vector.tensor_copy if g * HEAD_DIM < mine else nc.scalar.copy
-                regroup(copy, grouped[:, cols, :], head_raw[i][:, g, :, :])
+            mine //= HEAD_DIM
+            if mine:
+                regroup_passes(nc.vector.tensor_copy, grouped, head_raw[i], 0, mine)
+            if count - by_tensor > mine:
+                regroup_passes(nc.scalar.copy, grouped, head_raw[i], mine, count - by_tensor)
             for k, stage in enumerate(head_stages[i]):
                 g = count - by_tensor + 2 * k
                 empty_stage(stage, grouped[:, g * HEAD_DIM : (g + 2) * HEAD_DIM, :])
@@ -368,16 +376,19 @@ def tile_groupropeattention_pa_k_kernel(tc, x, Wq, Wk, Wv, out_0, out_1, out_2):
         multiply_q(PASSES - 1)
         stage_head(0)
         rg(0)
+        stage_head(1)
+        rg(1)
         for i in range(BATCH * UNIT // BANK):
             rope_q(i)
             if i:
                 rope_sum(nc.vector, *rope_q_out[i - 1])
+            if i == K0_AFTER:
+                qm(0)
         rope_sum(nc.vector, *rope_q_out[i])
-        for i in range(1, len(HEADS)):
+        for i in range(2, len(HEADS)):
             stage_head(i)
             rg(i)
-        v_acc.extend([psum.tile([P, HEAD_DIM], F32, name="v_acc", tag="bank_%d" % b) for b in range(BATCH)])
-        qm(0)
+        v_acc.extend([psum.tile([P, HEAD_DIM], F32, name="v_acc", tag="bank_%d" % (2 + b)) for b in range(BATCH)])
         qm(1)
         qm(2)
         qm(3)

@@ -31,18 +31,21 @@ HEADS = (
     (0, 8, 8, 0, 4),
     (1, 0, 8, 0, 4),
     (1, 8, 4, 128, 2),
-    (1, 12, 4, 128, 2),
+    (1, 12, 2, 0, 0),
+    (1, 14, 2, 128, 0),
 )
 RUN = 4
 WQ_AHEAD = 6
-VECTOR_COLS = 544
-LAST_VECTOR_COLS = 512
+VECTOR_COLS = 576
+LAST_VECTOR_COLS = 576
 FIRST_TENSOR_PASS = 12
-LATE_VECTOR_COLS = 448
-TENSOR_COLS = 256
+LATE_VECTOR_COLS = 384
+TENSOR_COLS = 128
 X_EVERY = 3
 STAGE_BANKS = (6, 7, 0, 1)
 K0_AFTER = 1
+X_STEPS = (1, 2, 4, 5, 7, 8, 10, 11)
+HEAD_UNIT = 8
 ROUND = 1.5 * 2.0**23
 
 FLOPS = 2 * BATCH * SEQ * EMB * (Q_HEADS + 2) * HEAD_DIM
@@ -56,10 +59,11 @@ def tile_groupropeattention_pa_k_kernel(tc, x, Wq, Wk, Wv, out_0, out_1, out_2):
     with ExitStack() as ctx:
         ctx.enter_context(tc.manual_schedule())
         const = ctx.enter_context(tc.tile_pool(name="const", bufs=1))
+        tail_pool = ctx.enter_context(tc.tile_pool(name="tail_pool", bufs=1))
         x_in = ctx.enter_context(tc.tile_pool(name="x_in", bufs=2 * CHUNKS))
         head_in = ctx.enter_context(tc.tile_pool(name="head_in", bufs=1))
         wide_in = ctx.enter_context(tc.tile_pool(name="wide_in", bufs=WQ_AHEAD))
-        w_grouped_pool = ctx.enter_context(tc.tile_pool(name="w_grouped_pool", bufs=5))
+        w_grouped_pool = ctx.enter_context(tc.tile_pool(name="w_grouped_pool", bufs=4))
         x_grouped_pool = ctx.enter_context(tc.tile_pool(name="x_grouped_pool", bufs=2))
         mx_pool = ctx.enter_context(tc.tile_pool(name="mx", bufs=5))
         rope_pool = ctx.enter_context(tc.tile_pool(name="rope", bufs=4))
@@ -76,8 +80,7 @@ def tile_groupropeattention_pa_k_kernel(tc, x, Wq, Wk, Wv, out_0, out_1, out_2):
         wq_raw = []
 
         def x_piece_behind(c):
-            chunk, b = c // X_EVERY, c % X_EVERY - 1
-            return (chunk, b) if chunk < CHUNKS and b >= 0 else None
+            return divmod(X_STEPS.index(c), BATCH) if c in X_STEPS else None
 
         def load_wq(c):
             raw = wide_in.tile([P, PACK, UNIT], BF16, name="wq_raw")
@@ -330,7 +333,10 @@ def tile_groupropeattention_pa_k_kernel(tc, x, Wq, Wk, Wv, out_0, out_1, out_2):
 
         def regroup_head(i):
             matrix, first, count, mine, by_tensor = HEADS[i]
-            grouped = w_grouped_pool.tile([P, UNIT, PACK], BF16, name="w_grouped", align_bytes=64)
+            if count == HEAD_UNIT:
+                grouped = w_grouped_pool.tile([P, UNIT, PACK], BF16, name="w_grouped", align_bytes=64)
+            else:
+                grouped = tail_pool.tile([P, count * HEAD_DIM, PACK], BF16, name="tail_grouped", tag="tail_grouped_%d" % i, align_bytes=64)
             mine //= HEAD_DIM
             if mine:
                 regroup_passes(nc.vector.tensor_copy, grouped, head_raw[i], 0, mine)
@@ -395,7 +401,8 @@ def tile_groupropeattention_pa_k_kernel(tc, x, Wq, Wk, Wv, out_0, out_1, out_2):
         rope_k = [rope_products(k_acc[b], 1) for b in range(BATCH)]
         for b in range(BATCH):
             rope_sum(nc.vector, rope_k[b], out_1[b].unsqueeze(1))
-        qm(4)
+        for i in range(4, len(HEADS)):
+            qm(i)
 
         for b in range(BATCH):
             value = rope_pool.tile([P, HEAD_DIM], F32, name="value")

@@ -34,7 +34,7 @@ HEADS = (
     (1, 12, 2, 0, 0),
     (1, 14, 2, 128, 0),
 )
-RUN = 4
+RUN = 2
 WQ_AHEAD = 6
 VECTOR_COLS = 576
 LAST_VECTOR_COLS = 576

import math
from contextlib import ExitStack

import concourse.mybir as mybir
from concourse.masks import make_identity

F32 = mybir.dt.float32
BF16 = mybir.dt.bfloat16
I32 = mybir.dt.int32
U32 = mybir.dt.uint32
U8 = mybir.dt.uint8
FP8X4 = mybir.dt.float8_e4m3fn_x4
ALU = mybir.AluOpType
ACT = mybir.ActivationFunctionType

BATCH, SEQ, EMB, HEAD_DIM, Q_HEADS = 2, 128, 8192, 128, 8
THETA = 10000.0
PAIRS = HEAD_DIM // 2
PAIR_BITS = 6

P = 128
PACK = 4
K_PASS = P * PACK
PASSES = EMB // K_PASS
BANK = 512
UNIT = 1024
GROUP = 4
CHUNKS = PASSES // GROUP
HEADS = (
    (0, 0, 8, 0, 0),
    (0, 8, 8, 0, 4),
    (1, 0, 8, 0, 4),
    (1, 8, 4, 128, 2),
    (1, 12, 2, 0, 0),
    (1, 14, 2, 128, 0),
)
RUN = 2
WQ_AHEAD = 6
VECTOR_COLS = 576
LAST_VECTOR_COLS = 576
FIRST_TENSOR_PASS = 12
LATE_VECTOR_COLS = 384
TENSOR_COLS = 128
X_EVERY = 3
STAGE_BANKS = (6, 7, 0, 1)
K0_AFTER = 1
X_STEPS = (1, 2, 4, 5, 7, 8, 10, 11)
HEAD_UNIT = 8
ROUND = 1.5 * 2.0**23

FLOPS = 2 * BATCH * SEQ * EMB * (Q_HEADS + 2) * HEAD_DIM

assert 2**PAIR_BITS == PAIRS
assert GROUP * BATCH * SEQ == UNIT and Q_HEADS * HEAD_DIM == UNIT


def tile_groupropeattention_pa_k_kernel(tc, x, Wq, Wk, Wv, out_0, out_1, out_2):
    nc = tc.nc
    with ExitStack() as ctx:
        ctx.enter_context(tc.manual_schedule())
        const = ctx.enter_context(tc.tile_pool(name="const", bufs=1))
        tail_pool = ctx.enter_context(tc.tile_pool(name="tail_pool", bufs=1))
        x_in = ctx.enter_context(tc.tile_pool(name="x_in", bufs=2 * CHUNKS))
        head_in = ctx.enter_context(tc.tile_pool(name="head_in", bufs=1))
        wide_in = ctx.enter_context(tc.tile_pool(name="wide_in", bufs=WQ_AHEAD))
        w_grouped_pool = ctx.enter_context(tc.tile_pool(name="w_grouped_pool", bufs=4))
        x_grouped_pool = ctx.enter_context(tc.tile_pool(name="x_grouped_pool", bufs=2))
        mx_pool = ctx.enter_context(tc.tile_pool(name="mx", bufs=5))
        rope_pool = ctx.enter_context(tc.tile_pool(name="rope", bufs=4))
        psum = ctx.enter_context(tc.psum_pool(name="psum", bufs=1))

        x_raw = {}

        def load_x(chunk, b):
            piece = x_in.tile([P, GROUP * K_PASS], BF16, name="x_raw")
            nc.sync.dma_start(out=piece[:], in_=x[b, :, chunk * GROUP * K_PASS : (chunk + 1) * GROUP * K_PASS])
            x_raw[chunk, b] = piece

        wq_passes = Wq.rearrange("(c p j) n -> c p (j n)", p=P, j=PACK)
        wq_raw = []

        def x_piece_behind(c):
            return divmod(X_STEPS.index(c), BATCH) if c in X_STEPS else None

        def load_wq(c):
            raw = wide_in.tile([P, PACK, UNIT], BF16, name="wq_raw")
            nc.sync.dma_start(out=raw[:].rearrange("p j n -> p (j n)"), in_=wq_passes[c])
            wq_raw.append(raw)
            if x_piece_behind(c):
                load_x(*x_piece_behind(c))

        for c in range(WQ_AHEAD):
            load_wq(c)

        warm = const.tile([P, 1], F32, name="warm")
        nc.vector.memset(warm[:], 0.0)
        warm_sin = const.tile([P, 1], F32, name="warm_sin")
        nc.scalar.activation(out=warm_sin[:], in_=warm[:], func=ACT.Sin)
        position = const.tile([P, 1], I32, name="position")
        nc.gpsimd.iota(position[:], pattern=[[0, 1]], base=0, channel_multiplier=1)
        ident = const.tile([P, P], F32, name="ident")
        make_identity(nc, ident[:])
        ident_bf16 = const.tile([P, P], BF16, name="ident_bf16")
        make_identity(nc, ident_bf16[:])

        position_turns = const.tile([P, 1], F32, name="position_turns")
        frequency = const.tile([P, PAIRS], F32, name="frequency")
        nc.vector.memset(frequency[:], 1.0)
        for level in range(PAIR_BITS):
            bit = 2**level
            bit_set = frequency[:].rearrange("p (a two s) -> p a two s", two=2, s=bit)[:, :, 1, :]
            nc.vector.tensor_scalar_mul(out=bit_set, in0=bit_set, scalar1=THETA ** (-bit / PAIRS))
        nc.vector.tensor_scalar_mul(out=position_turns[:], in0=position[:], scalar1=1.0 / (2.0 * math.pi))
        trig = const.tile([P, 3, PAIRS], F32, name="trig")
        cos, sin, minus_sin = trig[:, 0, :], trig[:, 1, :], trig[:, 2, :]

        def make_trig():
            turns = const.tile([P, 3, PAIRS], F32, name="turns")
            for row, shift in enumerate((0.25, 0.0, 0.5)):
                nc.vector.tensor_scalar(
                    out=turns[:, row, :],
                    in0=frequency[:],
                    scalar1=position_turns[:, 0:1],
                    scalar2=shift,
                    op0=ALU.mult,
                    op1=ALU.add,
                )
            whole_turns = const.tile([P, 3, PAIRS], F32, name="whole_turns")
            nc.vector.tensor_scalar(
                out=whole_turns[:], in0=turns[:], scalar1=ROUND, scalar2=ROUND, op0=ALU.add, op1=ALU.subtract
            )
            nc.vector.tensor_tensor(out=turns[:], in0=turns[:], in1=whole_turns[:], op=ALU.subtract)
            nc.scalar.activation(out=trig[:], in_=turns[:], func=ACT.Sin, scale=2.0 * math.pi)

        def quantise(grouped, codes, scales):
            nc.vector.quantize_mx(out=codes.bitcast(FP8X4), scales=scales, in_=grouped)

        def quantise_weights(grouped, parts):
            codes = mx_pool.tile([P, UNIT], U32, name="w_codes", align_bytes=64)
            scales = mx_pool.tile([P, UNIT], U8, name="w_scales", align_bytes=64)
            width = UNIT // parts
            for i in range(parts):
                cols = slice(i * width, (i + 1) * width)
                quantise(grouped[:, cols, :].rearrange("p n j -> p (n j)"), codes[:, cols], scales[:, cols])
            return codes, scales

        def regroup(copy, grouped_cols, raw_cols):
            copy(
                out=grouped_cols.rearrange("p (c i) j -> p c j i", i=RUN),
                in_=raw_cols.rearrange("p j (c i) -> p c j i", i=RUN),
            )

        def multiply(acc, c, b, codes, scales, cols):
            tokens = slice((c * BATCH + b) * SEQ, (c * BATCH + b + 1) * SEQ)
            nc.tensor.matmul_mx(
                out=acc[:],
                lhsT=x_codes[:, tokens].bitcast(FP8X4),
                lhsT_scale=x_scales[:, tokens],
                rhs=codes[:, cols].bitcast(FP8X4),
                rhs_scale=scales[:, cols],
                start=(c == 0),
                stop=(c == PASSES - 1),
            )

        def rope_products(acc, heads):
            pairs = acc[:].rearrange("p (h k two) -> p h k two", h=heads, two=2)
            direct = rope_pool.tile([P, heads, PAIRS, 2], F32, name="direct")
            nc.vector.tensor_tensor(
                out=direct[:],
                in0=pairs,
                in1=cos.unsqueeze(1).unsqueeze(3).to_broadcast([P, heads, PAIRS, 2]),
                op=ALU.mult,
            )
            crossed = rope_pool.tile([P, heads, 2, PAIRS], F32, name="crossed")
            nc.vector.tensor_tensor(
                out=crossed[:, :, 0, :],
                in0=pairs[:, :, :, 1],
                in1=minus_sin.unsqueeze(1).to_broadcast([P, heads, PAIRS]),
                op=ALU.mult,
            )
            nc.vector.tensor_tensor(
                out=crossed[:, :, 1, :],
                in0=pairs[:, :, :, 0],
                in1=sin.unsqueeze(1).to_broadcast([P, heads, PAIRS]),
                op=ALU.mult,
            )
            return direct, crossed

        def rope_sum(engine, products, out_rows):
            direct, crossed = products
            engine.tensor_tensor(
                out=direct[:], in0=direct[:], in1=crossed[:].rearrange("p h two k -> p h k two"), op=ALU.add
            )
            nc.sync.dma_start(out=out_rows, in_=direct[:].rearrange("p h k two -> p h (k two)"))

        x_codes = const.tile([P, PASSES * BATCH * SEQ], U32, name="x_codes", align_bytes=64)
        x_scales = const.tile([P, PASSES * BATCH * SEQ], U8, name="x_scales", align_bytes=64)
        x_grouped = {}

        x_banks = {}

        def transpose_x(chunk, b):
            words = x_raw[chunk, b][:].bitcast(F32).rearrange("t (g p u) -> t g u p", g=GROUP, u=2)
            for first in range(0, GROUP, 2):
                bank = psum.tile([P, 2, 2, SEQ], F32, name="x_bank", tag="bank_%d" % (4 + 2 * b + first // 2))
                for u in range(2):
                    for g in range(2):
                        nc.tensor.transpose(out=bank[:, u, g, :], in_=words[:, first + g, u, :], identity=ident[:])
                x_banks[chunk, b, first] = bank

        def copy_x(chunk, b):
            if b == 0:
                x_grouped[chunk] = x_grouped_pool.tile([P, UNIT * PACK], BF16, name="x_grouped", align_bytes=64)
            grouped = x_grouped[chunk][:].bitcast(F32).rearrange("p (g b t u) -> p g b t u", g=GROUP, b=BATCH, u=2)
            for first in range(0, GROUP, 2):
                bank = x_banks[chunk, b, first]
                nc.scalar.copy(out=grouped[:, first : first + 2, b, :, :], in_=bank[:].rearrange("p u g t -> p g t u"))

        def quantise_x(chunk):
            cols = slice(chunk * UNIT, (chunk + 1) * UNIT)
            quantise(x_grouped[chunk][:], x_codes[:, cols], x_scales[:, cols])

        q_acc = [psum.tile([P, BANK], F32, name="q_acc", tag="bank_%d" % i) for i in range(BATCH * UNIT // BANK)]

        stages = []

        def regroup_by_tensor(pieces, bank):
            stage = psum.tile([P, len(pieces), HEAD_DIM, PACK], BF16, name="stage", tag="bank_%d" % bank)
            stages.append(stage)
            for k, raw in enumerate(pieces):
                nc.tensor.matmul(
                    out=stage[:, k, :, :].rearrange("p n j -> p j n"), lhsT=ident_bf16[:], rhs=raw, start=True, stop=True
                )
            return stage

        def empty_stage(stage, grouped_cols):
            nc.scalar.copy(
                out=grouped_cols.rearrange("p n j -> p (n j)"), in_=stage[:].rearrange("p k n j -> p (k n j)")
            )

        wq_stages = {}

        def stage_wq(c):
            if FIRST_TENSOR_PASS <= c < PASSES - 1:
                starts = range(UNIT - TENSOR_COLS, UNIT, HEAD_DIM)
                wq_stages[c] = regroup_by_tensor([wq_raw[c][:, :, i : i + HEAD_DIM] for i in starts], 6 + c % 2)

        def regroup_wq(c):
            grouped = w_grouped_pool.tile([P, UNIT, PACK], BF16, name="w_grouped", align_bytes=64)
            raw = wq_raw[c]
            if c < PASSES - 1:
                helped = c >= FIRST_TENSOR_PASS
                a, b = (LATE_VECTOR_COLS, UNIT - TENSOR_COLS) if helped else (VECTOR_COLS, UNIT)
                regroup(nc.vector.tensor_copy, grouped[:, :a, :], raw[:, :, :a])
                regroup(nc.scalar.copy, grouped[:, a:b, :], raw[:, :, a:b])
                if helped:
                    empty_stage(wq_stages[c], grouped[:, b:, :])
            else:
                for first in range(0, UNIT, UNIT // 2):
                    a, b = first + LAST_VECTOR_COLS // 2, first + UNIT // 2
                    regroup(nc.vector.tensor_copy, grouped[:, first:a, :], raw[:, :, first:a])
                    regroup(nc.scalar.copy, grouped[:, a:b, :], raw[:, :, a:b])
            if c + WQ_AHEAD < PASSES:
                load_wq(c + WQ_AHEAD)
            return grouped

        quantised = {}

        def multiply_q(c):
            for half in range(UNIT // BANK):
                for b in range(BATCH):
                    cols = slice(half * BANK, (half + 1) * BANK)
                    multiply(q_acc[half * BATCH + b], c, b, *quantised[c], cols)

        grouped = {}
        multiplied = 0
        for c in range(PASSES):
            if c == PASSES - 1:
                quantised[c - 1] = quantise_weights(grouped[c - 1], 1)
            grouped[c] = regroup_wq(c)
            piece = x_piece_behind(c)
            if piece:
                copy_x(*piece)
            if c + 1 < PASSES and x_piece_behind(c + 1):
                transpose_x(*x_piece_behind(c + 1))
            stage_wq(c + 1)
            if c == 0:
                continue
            if c == 1:
                make_trig()
            if c < PASSES - 1:
                quantised[c - 1] = quantise_weights(grouped[c - 1], 1)
            done = x_piece_behind(c - 1)
            if done and done[1] == BATCH - 1:
                quantise_x(done[0])
                x_ready = (done[0] + 1) * GROUP
            for turn in range(2):
                if c >= X_EVERY and multiplied < min(c, x_ready):
                    multiply_q(multiplied)
                    multiplied += 1

        head_raw = []
        for i, (matrix, first, count, mine, by_tensor) in enumerate(HEADS):
            raw = head_in.tile([P, count, PACK, HEAD_DIM], BF16, name="head_raw", tag="head_raw_%d" % i)
            rows = (Wk, Wv)[matrix][first * K_PASS : (first + count) * K_PASS, :]
            nc.sync.dma_start(
                out=raw[:].rearrange("p g j n -> p g (j n)"),
                in_=rows.rearrange("(g p j) n -> p g (j n)", p=P, j=PACK),
            )
            head_raw.append(raw)
        k_acc = [psum.tile([P, HEAD_DIM], F32, name="k_acc", tag="bank_%d" % (4 + b)) for b in range(BATCH)]
        v_acc = []

        head_stages = {}

        def stage_bank():
            used.append(0)
            return STAGE_BANKS[(len(used) - 1) % len(STAGE_BANKS)]

        used = []

        def stage_head(i):
            matrix, first, count, mine, by_tensor = HEADS[i]
            head_stages[i] = [
                regroup_by_tensor([head_raw[i][:, g + k, :, :] for k in range(2)], stage_bank()) for g in range(count - by_tensor, count, 2)
            ]

        def regroup_passes(copy, grouped, raw, first, end):
            copy(
                out=grouped[:, first * HEAD_DIM : end * HEAD_DIM, :].rearrange("p (g c i) j -> p g c j i", c=HEAD_DIM // RUN, i=RUN),
                in_=raw[:, first:end, :, :].rearrange("p g j (c i) -> p g c j i", i=RUN),
            )

        def regroup_head(i):
            matrix, first, count, mine, by_tensor = HEADS[i]
            if count == HEAD_UNIT:
                grouped = w_grouped_pool.tile([P, UNIT, PACK], BF16, name="w_grouped", align_bytes=64)
            else:
                grouped = tail_pool.tile([P, count * HEAD_DIM, PACK], BF16, name="tail_grouped", tag="tail_grouped_%d" % i, align_bytes=64)
            mine //= HEAD_DIM
            if mine:
                regroup_passes(nc.vector.tensor_copy, grouped, head_raw[i], 0, mine)
            if count - by_tensor > mine:
                regroup_passes(nc.scalar.copy, grouped, head_raw[i], mine, count - by_tensor)
            for k, stage in enumerate(head_stages[i]):
                g = count - by_tensor + 2 * k
                empty_stage(stage, grouped[:, g * HEAD_DIM : (g + 2) * HEAD_DIM, :])
            return grouped

        def quantise_head(i, grouped):
            width = HEADS[i][2] * HEAD_DIM
            codes = mx_pool.tile([P, UNIT], U32, name="w_codes", align_bytes=64)
            scales = mx_pool.tile([P, UNIT], U8, name="w_scales", align_bytes=64)
            quantise(grouped[:, :width, :].rearrange("p n j -> p (n j)"), codes[:, :width], scales[:, :width])
            return codes, scales

        def multiply_head(i, codes, scales):
            matrix, first, count, mine, by_tensor = HEADS[i]
            for g in range(count):
                for b in range(BATCH):
                    cols = slice(g * HEAD_DIM, (g + 1) * HEAD_DIM)
                    multiply((k_acc, v_acc)[matrix][b], first + g, b, codes, scales, cols)

        heads_in_bank = BANK // HEAD_DIM

        rope_q_out = {}

        def rope_q(i):
            half, b = divmod(i, BATCH)
            heads = slice(half * heads_in_bank, (half + 1) * heads_in_bank)
            rope_q_out[i] = (rope_products(q_acc[i], heads_in_bank), out_0[b, heads].rearrange("h t d -> t h d"))

        head_grouped = {}

        def rg(i):
            head_grouped[i] = regroup_head(i)

        def qm(i):
            multiply_head(i, *quantise_head(i, head_grouped[i]))

        quantised[PASSES - 1] = quantise_weights(grouped[PASSES - 1], 2)
        multiply_q(PASSES - 1)
        stage_head(0)
        rg(0)
        stage_head(1)
        rg(1)
        for i in range(BATCH * UNIT // BANK):
            rope_q(i)
            if i:
                rope_sum(nc.vector, *rope_q_out[i - 1])
            if i == K0_AFTER:
                qm(0)
        rope_sum(nc.vector, *rope_q_out[i])
        for i in range(2, len(HEADS)):
            stage_head(i)
            rg(i)
        v_acc.extend([psum.tile([P, HEAD_DIM], F32, name="v_acc", tag="bank_%d" % (2 + b)) for b in range(BATCH)])
        qm(1)
        qm(2)
        qm(3)
        rope_k = [rope_products(k_acc[b], 1) for b in range(BATCH)]
        for b in range(BATCH):
            rope_sum(nc.vector, rope_k[b], out_1[b].unsqueeze(1))
        for i in range(4, len(HEADS)):
            qm(i)

        for b in range(BATCH):
            value = rope_pool.tile([P, HEAD_DIM], F32, name="value")
            nc.scalar.copy(out=value[:], in_=v_acc[b][:])
            nc.sync.dma_start(out=out_2[b], in_=value[:])
